import numpy as np
import ml_dtypes


def mxq(x, axis, fmt="e4m3"):
    dtype, down = {"e4m3": (ml_dtypes.float8_e4m3fn, 7), "e5m2": (ml_dtypes.float8_e5m2, 14)}[fmt]
    v = np.moveaxis(np.asarray(x, np.float32).astype(ml_dtypes.bfloat16).astype(np.float64), axis, -1)
    blocks = v.reshape(v.shape[:-1] + (-1, 32))
    amax = np.abs(blocks).max(-1, keepdims=True)
    byte = np.maximum(np.where(amax > 0, np.frexp(amax)[1] - 1 + 127, 0) - down, 1)
    scale = np.exp2(byte - 127.0)
    codes = (blocks / scale).astype(np.float32).astype(dtype).astype(np.float64)
    return np.moveaxis((codes * scale).reshape(v.shape), -1, axis)


WIDE = False


def mx_kscale(k):
    if not WIDE:
        return np.ones(k)
    levels = np.array([18, -18])
    if k % 512:
        return np.exp2(np.random.permutation(np.resize(levels, k // 32))).repeat(32)
    a = np.empty((k // 512, 16))
    for p in range(k // 512):
        a[p, :8] = np.random.permutation(np.resize(levels, 8))
        for g in range(8):
            far = levels[np.abs(levels - a[p, g]) >= 10]
            a[p, g + 8] = far[np.random.randint(len(far))]
    return np.exp2(a.ravel()).repeat(32)


BF16 = ml_dtypes.bfloat16


def bf(x):
    return np.asarray(x, np.float32).astype(BF16)


def f64(x):
    return np.asarray(x).astype(np.float64)


G, NSPIN, D_ONE, D_TWO = 96, 8, 512, 256
N = 2 * G * NSPIN
K1 = D_ONE + 2 * D_TWO
K2 = 2 * D_ONE
TANH_GAIN = 1.5927812698663606


def joined_features(h_one, h_two_same, h_two_diff):
    pair_same = f64(h_two_same).reshape(N, NSPIN, D_TWO).mean(axis=1)
    pair_diff = f64(h_two_diff).reshape(N, NSPIN, D_TWO).mean(axis=1)
    return np.concatenate([f64(h_one), pair_same, pair_diff], axis=-1)


def pre_activation(h_one, h_two_same, h_two_diff, W1, b1, Wg):
    g_mean = f64(h_one).reshape(G, 2, NSPIN, D_ONE).mean(axis=2)
    g_inp = np.stack([
        np.concatenate([g_mean[:, 0], g_mean[:, 1]], axis=-1),
        np.concatenate([g_mean[:, 1], g_mean[:, 0]], axis=-1),
    ], axis=1).reshape(2 * G, K2)
    a = joined_features(h_one, h_two_same, h_two_diff) @ f64(W1) + f64(b1)
    return a + np.repeat(g_inp @ f64(Wg), NSPIN, axis=0)


def setup_inputs():
    s = mx_kscale(N)
    u = mx_kscale(D_ONE)
    s_pair = np.repeat(s, NSPIN)[:, None]
    w10 = bf(np.random.standard_normal((K1, D_ONE)) / np.sqrt(K1))
    h0 = bf(np.random.standard_normal((N, D_ONE)))
    same0 = bf(np.random.standard_normal((N * NSPIN, D_TWO)) * 2.0)
    diff0 = bf(np.random.standard_normal((N * NSPIN, D_TWO)) * 2.0)
    b1 = bf(np.random.standard_normal(D_ONE) * 0.3)
    wg = bf(np.random.standard_normal((K2, D_ONE)) * 2.0 / np.sqrt(K2))
    g = bf(np.random.standard_normal((N, D_ONE)) * np.exp2(np.random.randint(-6, 1, (N, 1))) * 8.0 / s[:, None] * u)
    z = pre_activation(h0, same0, diff0, w10, b1, wg)
    return {"h_one": bf(f64(h0) * s[:, None]),
            "h_two_same": bf(f64(same0) * s_pair),
            "h_two_diff": bf(f64(diff0) * s_pair),
            "W1": bf(f64(w10) / u),
            "b1": b1,
            "Wg": wg,
            "z": np.asarray(z, np.float32),
            "grad_out": g}


def reference(h_one, h_two_same, h_two_diff, W1, b1, Wg, z, grad_out):
    t = np.tanh(f64(z) / np.sqrt(2.0))
    dz = f64(grad_out) * (0.5 * TANH_GAIN * (1.0 - t * t))
    w_same = f64(W1)[D_ONE:D_ONE + D_TWO]
    d_pair = mxq(dz, 1, "e5m2") @ mxq(w_same, 1, "e4m3").T
    d_same = np.repeat(d_pair / NSPIN, NSPIN, axis=0)
    one_in = joined_features(h_one, h_two_same, h_two_diff)
    dw1 = mxq(one_in, 0, "e4m3").T @ mxq(dz, 0, "e5m2")
    return d_same, dw1

@@ -1,0 +1,289 @@
+import math
+from contextlib import ExitStack
+
+import concourse.mybir as mybir
+from concourse.masks import make_identity
+
+N_ELEC, N_SPIN, D_ONE, D_TWO = 1536, 8, 512, 256
+K_IN = D_ONE + 2 * D_TWO
+DZ_GAIN = 0.5 * 1.5927812698663606
+
+FLOPS = 2 * N_ELEC * D_ONE * D_TWO + 2 * N_ELEC * K_IN * D_ONE
+BYTES = (
+    2 * N_ELEC * D_ONE * 2
+    + N_ELEC * D_ONE * 4
+    + 2 * N_ELEC * N_SPIN * D_TWO * 2
+    + D_TWO * D_ONE * 2
+    + N_ELEC * N_SPIN * D_TWO * 4
+    + K_IN * D_ONE * 4
+)
+
+F32 = mybir.dt.float32
+BF16 = mybir.dt.bfloat16
+U32 = mybir.dt.uint32
+U8 = mybir.dt.uint8
+E4M3 = mybir.dt.float8_e4m3fn_x4
+E5M2 = mybir.dt.float8_e5m2_x4
+ACT = mybir.ActivationFunctionType
+ALU = mybir.AluOpType
+
+P = 128
+PACK = 4
+K_PASS = P * PACK
+PASSES = N_ELEC // K_PASS
+BANK = 512
+HALF_ROWS = N_SPIN // 2
+F_BLOCKS = D_TWO // P
+CHUNKS = 2 * PASSES * 2
+PAIR_BUFS = 10
+
+
+def tile_fermilayer_pa_v_kernel(
+    tc, h_one, h_two_same, h_two_diff, W1, b1, Wg, z, grad_out, out_0, out_1
+):
+    nc = tc.nc
+
+    z_hbm = z.rearrange("(g p j) c -> g p (j c)", p=P, j=PACK)
+    grad_hbm = grad_out.rearrange("(g p j) c -> g p (j c)", p=P, j=PACK)
+    h_hbm = h_one.rearrange("(g p j) c -> g p (j c)", p=P, j=PACK)
+    pair_hbm = [
+        stream.rearrange("(g p u x) f -> g u p (x f)", p=P, u=2, x=2 * N_SPIN)
+        for stream in (h_two_same, h_two_diff)
+    ]
+    w_hbm = W1[D_ONE : D_ONE + D_TWO, :].rearrange("(a r) k -> r a k", r=P)
+    out0_hbm = out_0.rearrange("(g p j q r) f -> g j p q (r f)", p=P, j=PACK, r=2, q=N_SPIN // 2)
+    out1_hbm = out_1.rearrange("(q a p) c -> q p a c", a=2, p=P)
+
+    with ExitStack() as ctx:
+        keep = ctx.enter_context(tc.tile_pool(name="keep", bufs=1))
+        work = ctx.enter_context(tc.tile_pool(name="work", bufs=2))
+        psum = ctx.enter_context(tc.psum_pool(name="psum", bufs=2))
+        ctx.enter_context(tc.manual_schedule())
+
+        ident = keep.tile([P, P], F32)
+        make_identity(nc, ident[:])
+
+        w_codes = keep.tile([P, BANK], U32, align_bytes=64)
+        w_scales = keep.tile([P, BANK], U8, align_bytes=64)
+        dz_codes = [keep.tile([P, D_ONE], U32, align_bytes=64, name="dz_codes%d" % g) for g in range(PASSES)]
+        dz_scales = [keep.tile([P, D_ONE], U8, align_bytes=64, name="dz_scales%d" % g) for g in range(PASSES)]
+        in_codes = [keep.tile([P, K_IN], U32, align_bytes=64, name="in_codes%d" % g) for g in range(PASSES)]
+        in_scales = [keep.tile([P, K_IN], U8, align_bytes=64, name="in_scales%d" % g) for g in range(PASSES)]
+
+        z_sb, grad_sb, h_sb, pair_sb = {}, {}, {}, {}
+        dz_sb, dz_tok, dz_feat, dzt_codes, dzt_scales = {}, {}, {}, {}, {}
+        part_sb, mean_t, back_ps, mean_tok, h_tok = {}, {}, {}, {}, {}
+
+        def load_z(g):
+            z_sb[g] = work.tile([P, PACK * D_ONE], F32, tag="wide", bufs=PASSES, name="z_sb")
+            nc.sync.dma_start(out=z_sb[g][:], in_=z_hbm[g])
+
+        def load_grad(g):
+            grad_sb[g] = work.tile([P, PACK * D_ONE], BF16, tag="narrow", bufs=2 * PASSES, name="grad_sb")
+            nc.sync.dma_start(out=grad_sb[g][:], in_=grad_hbm[g])
+
+        def load_h(g):
+            h_sb[g] = work.tile([P, PACK * D_ONE], BF16, tag="narrow", bufs=2 * PASSES, name="h_sb")
+            nc.sync.dma_start(out=h_sb[g][:], in_=h_hbm[g])
+
+        def load_pair(n):
+            stream, g, u = n // (2 * PASSES), n // 2 % PASSES, n % 2
+            pair_sb[n] = work.tile([P, 2 * N_SPIN * D_TWO], BF16, tag="pair", bufs=PAIR_BUFS, name="pair_sb")
+            nc.sync.dma_start(out=pair_sb[n][:], in_=pair_hbm[stream][g, u])
+
+        def grouped_tile(name):
+            grouped = work.tile([P, PACK * D_ONE], BF16, tag="grouped", bufs=3, align_bytes=64, name=name)
+            return grouped
+
+        def weight_operand(w_sb):
+            words = w_sb[:].rearrange("p a k -> p (a k)").bitcast(F32)
+            bank = psum.tile([P, BANK], F32, tag="turn", name="w_bank")
+            for a in range(F_BLOCKS):
+                for u in range(2):
+                    col = (2 * a + u) * P
+                    nc.tensor.transpose(bank[:, col : col + P], words[:, 2 * P * a + u : 2 * P * (a + 1) : 2], ident[:])
+            w_grouped = grouped_tile("w_grouped")
+            for rep in range(2):
+                dst = w_grouped[:].bitcast(F32)[:, rep * BANK : (rep + 1) * BANK]
+                nc.scalar.copy(
+                    out=dst.rearrange("p (a r u) -> p a r u", a=F_BLOCKS, u=2),
+                    in_=bank[:].rearrange("p (a u r) -> p a r u", a=F_BLOCKS, u=2),
+                )
+            return w_grouped
+
+        def dz_activations(g):
+            nc.scalar.activation(out=z_sb[g][:], in_=z_sb[g][:], func=ACT.Tanh, scale=1.0 / math.sqrt(2.0))
+            nc.scalar.activation(out=z_sb[g][:], in_=z_sb[g][:], func=ACT.Square, scale=math.sqrt(DZ_GAIN))
+
+        def dz_round(g):
+            dz_sb[g] = work.tile([P, PACK * D_ONE], BF16, tag="dz", name="dz_sb")
+            nc.vector.scalar_tensor_tensor(
+                out=dz_sb[g][:], in0=z_sb[g][:], scalar=DZ_GAIN, in1=grad_sb[g][:], op0=ALU.subtract, op1=ALU.mult
+            )
+
+        def dz_layouts(g):
+            dz_tok[g] = grouped_tile("dz_tok")
+            nc.vector.tensor_copy(
+                out=dz_tok[g][:].rearrange("p (c j) -> p c j", j=PACK),
+                in_=dz_sb[g][:].rearrange("p (j c) -> p c j", j=PACK),
+            )
+            words = dz_sb[g][:].bitcast(F32)
+            dz_feat[g] = grouped_tile("dz_feat")
+            for half in range(2):
+                bank = psum.tile([P, BANK], F32, tag="turn", name="dz_bank")
+                for e in range(2):
+                    j = 2 * half + e
+                    for u in range(2):
+                        col = (2 * e + u) * P
+                        nc.tensor.transpose(
+                            bank[:, col : col + P], words[:, 2 * P * j + u : 2 * P * (j + 1) : 2], ident[:]
+                        )
+                dst = dz_feat[g][:].bitcast(F32)[:, half * BANK : (half + 1) * BANK]
+                nc.scalar.copy(
+                    out=dst.rearrange("p (e r u) -> p e r u", e=2, u=2),
+                    in_=bank[:].rearrange("p (e u r) -> p e r u", e=2, u=2),
+                )
+
+        def dz_quantize(g):
+            nc.vector.quantize_mx(out=dz_codes[g][:].bitcast(E5M2), scales=dz_scales[g][:], in_=dz_tok[g][:])
+            dzt_codes[g] = work.tile([P, K_PASS], U32, tag="dzt_codes", align_bytes=64, name="dzt_codes")
+            dzt_scales[g] = work.tile([P, K_PASS], U8, tag="dzt_scales", align_bytes=64, name="dzt_scales")
+            nc.vector.quantize_mx(out=dzt_codes[g][:].bitcast(E5M2), scales=dzt_scales[g][:], in_=dz_feat[g][:])
+
+        def pair_gradient(g):
+            result = work.tile([P, PACK * BANK], F32, tag="wide", bufs=PASSES, name="d_pair")
+            for j in range(PACK):
+                acc = psum.tile([P, BANK], F32, tag="mx", name="acc0")
+                nc.tensor.matmul_mx(
+                    out=acc[:],
+                    lhsT=dzt_codes[g][:, j * P : (j + 1) * P].bitcast(E5M2),
+                    lhsT_scale=dzt_scales[g][:, j * P : (j + 1) * P],
+                    rhs=w_codes[:].bitcast(E4M3),
+                    rhs_scale=w_scales[:],
+                    start=True,
+                    stop=True,
+                )
+                twice = result[:, j * BANK : (j + 1) * BANK]
+                nc.scalar.activation(out=twice, in_=acc[:], func=ACT.Copy, scale=-1.0 / N_SPIN)
+                nc.sync.dma_start(out=out0_hbm[g, j], in_=twice.unsqueeze(1).to_broadcast([P, N_SPIN // 2, BANK]))
+
+        def pair_add(n):
+            rows = pair_sb[n][:].rearrange("p (e h x) -> p e h x", e=2, h=2)
+            part_sb[n] = work.tile([P, 2, HALF_ROWS * D_TWO], F32, tag="part", bufs=3, name="part_sb")
+            nc.vector.tensor_tensor(out=part_sb[n][:], in0=rows[:, :, 0, :], in1=rows[:, :, 1, :], op=ALU.add)
+
+        def pair_mean(n):
+            bank = psum.tile([P, BANK], F32, tag="sum", name="sum_bank")
+            for b in range(F_BLOCKS):
+                for e in range(2):
+                    col = (2 * b + e) * P
+                    for r in range(HALF_ROWS):
+                        first = r * D_TWO + b * P
+                        nc.tensor.matmul(
+                            bank[:, col : col + P],
+                            lhsT=part_sb[n][:, e, first : first + P],
+                            rhs=ident[:],
+                            is_transpose=True,
+                            start=(r == 0),
+                            stop=(r == HALF_ROWS - 1),
+                        )
+            mean_t[n] = work.tile([P, BANK], BF16, tag="mean_t", name="mean_t")
+            nc.scalar.activation(
+                out=mean_t[n][:].rearrange("p (b q e) -> p b q e", b=F_BLOCKS, e=2),
+                in_=bank[:].rearrange("p (b e q) -> p b q e", b=F_BLOCKS, e=2),
+                func=ACT.Copy,
+                scale=1.0 / N_SPIN,
+            )
+
+        def pair_turn_back(n):
+            k, u = divmod(n, 2)
+            if u == 0:
+                back_ps[k] = psum.tile([P, BANK], F32, tag="back", name="back_bank")
+            words = mean_t[n][:].bitcast(F32)
+            for b in range(F_BLOCKS):
+                col = u * D_TWO + b * P
+                nc.tensor.transpose(back_ps[k][:, col : col + P], words[:, b * P : (b + 1) * P], ident[:])
+            if u == 1:
+                mean_tok[k] = work.tile([P, PACK * D_TWO], BF16, tag="mean_tok", align_bytes=64, name="mean_tok")
+                nc.scalar.copy(
+                    out=mean_tok[k][:].bitcast(F32).rearrange("p (f u) -> p f u", u=2),
+                    in_=back_ps[k][:].rearrange("p (u f) -> p f u", u=2),
+                )
+
+        def pair_quantize(k):
+            stream, g = divmod(k, PASSES)
+            cols = slice(D_ONE + stream * D_TWO, D_ONE + (stream + 1) * D_TWO)
+            nc.vector.quantize_mx(out=in_codes[g][:, cols].bitcast(E4M3), scales=in_scales[g][:, cols], in_=mean_tok[k][:])
+
+        def h_interleave(g):
+            h_tok[g] = grouped_tile("h_tok")
+            nc.scalar.copy(
+                out=h_tok[g][:].rearrange("p (c j) -> p c j", j=PACK),
+                in_=h_sb[g][:].rearrange("p (j c) -> p c j", j=PACK),
+            )
+
+        def h_quantize(g):
+            nc.vector.quantize_mx(
+                out=in_codes[g][:, :D_ONE].bitcast(E4M3), scales=in_scales[g][:, :D_ONE], in_=h_tok[g][:]
+            )
+
+        def weight_gradient(q):
+            result = work.tile([P, 2, D_ONE], F32, tag="narrow", bufs=2 * PASSES, name="d_w")
+            for a in range(2):
+                cols = slice((2 * q + a) * P, (2 * q + a + 1) * P)
+                acc = psum.tile([P, BANK], F32, tag="mx", name="acc1")
+                for g in range(PASSES):
+                    nc.tensor.matmul_mx(
+                        out=acc[:],
+                        lhsT=in_codes[g][:, cols].bitcast(E4M3),
+                        lhsT_scale=in_scales[g][:, cols],
+                        rhs=dz_codes[g][:].bitcast(E5M2),
+                        rhs_scale=dz_scales[g][:],
+                        start=(g == 0),
+                        stop=(g == PASSES - 1),
+                    )
+                nc.scalar.activation(out=result[:, a, :], in_=acc[:], func=ACT.Copy, scale=-1.0)
+            nc.sync.dma_start(out=out1_hbm[q], in_=result[:])
+
+        w_sb = keep.tile([P, F_BLOCKS, D_ONE], BF16)
+        for g in range(PASSES):
+            load_pair(2 * g)
+            load_z(g)
+            load_grad(g)
+            if g == 0:
+                nc.sync.dma_start(out=w_sb[:], in_=w_hbm)
+            load_pair(2 * g + 1)
+        for g in range(PASSES):
+            load_h(g)
+        for n in range(2 * PASSES, PAIR_BUFS):
+            load_pair(n)
+
+        dz_stages = [dz_activations, dz_round, dz_layouts, dz_quantize, pair_gradient]
+        h_first = 2 * PASSES + 1
+        for step in range(CHUNKS + 3):
+            if step % 2 == 0 and step // 2 < PASSES:
+                dz_activations(step // 2)
+            if step < CHUNKS:
+                pair_add(step)
+            if step + PAIR_BUFS < CHUNKS:
+                load_pair(step + PAIR_BUFS)
+            if 0 <= step - 1 < CHUNKS:
+                pair_mean(step - 1)
+            if 0 <= step - 2 < CHUNKS:
+                pair_turn_back(step - 2)
+            if 0 <= step - 3 < CHUNKS and (step - 3) % 2 == 1:
+                pair_quantize((step - 3) // 2)
+            if step == 0:
+                w_grouped = weight_operand(w_sb)
+            if step == 1:
+                nc.vector.quantize_mx(out=w_codes[:].bitcast(E4M3), scales=w_scales[:], in_=w_grouped[:])
+            for g in range(PASSES):
+                if 1 <= step - 2 * g < len(dz_stages):
+                    dz_stages[step - 2 * g](g)
+            if 0 <= step - h_first - 1 < PASSES:
+                h_quantize(step - h_first - 1)
+            if 0 <= step - h_first < PASSES:
+                h_interleave(step - h_first)
+            if 0 <= step - h_first - PASSES - 1 < 3:
+                weight_gradient(step - h_first - PASSES - 1)
+        weight_gradient(3)

@@ -29,13 +29,22 @@ ALU = mybir.AluOpType
 
 P = 128
 PACK = 4
-K_PASS = P * PACK
-PASSES = N_ELEC // K_PASS
+PASSES = N_ELEC // (P * PACK)
 BANK = 512
-HALF_ROWS = N_SPIN // 2
+BANKS = 8
 F_BLOCKS = D_TWO // P
-CHUNKS = 2 * PASSES * 2
-PAIR_BUFS = 10
+PARTS = N_SPIN // 2
+ROW = PACK * D_ONE
+
+CHUNKS = 2 * PASSES
+HALVES = 2 * CHUNKS
+HALF = 2 * N_SPIN * D_TWO
+COPIES = 4
+
+DZ_FIRST = 1
+DZ_LEAD = 2
+W_STEP = 2
+H_FIRST = 8
 
 
 def tile_fermilayer_pa_v_kernel(
@@ -47,17 +56,17 @@ def tile_fermilayer_pa_v_kernel(
     grad_hbm = grad_out.rearrange("(g p j) c -> g p (j c)", p=P, j=PACK)
     h_hbm = h_one.rearrange("(g p j) c -> g p (j c)", p=P, j=PACK)
     pair_hbm = [
-        stream.rearrange("(g p u x) f -> g u p (x f)", p=P, u=2, x=2 * N_SPIN)
-        for stream in (h_two_same, h_two_diff)
+        stream.rearrange("(g p x) f -> g p (x f)", p=P, x=PACK * N_SPIN) for stream in (h_two_same, h_two_diff)
     ]
-    w_hbm = W1[D_ONE : D_ONE + D_TWO, :].rearrange("(a r) k -> r a k", r=P)
-    out0_hbm = out_0.rearrange("(g p j q r) f -> g j p q (r f)", p=P, j=PACK, r=2, q=N_SPIN // 2)
-    out1_hbm = out_1.rearrange("(q a p) c -> q p a c", a=2, p=P)
+    w_hbm = W1[D_ONE : D_ONE + D_TWO, :].rearrange("(r a) k -> r (a k)", r=P)
+    out0_hbm = out_0.rearrange("(g p j q r) f -> g j p q (r f)", p=P, j=PACK, q=N_SPIN // COPIES, r=COPIES)
+    out1_h = out_1[:D_ONE, :].rearrange("(a p) c -> p a c", p=P)
+    out1_pair = out_1[D_ONE:, :].rearrange("(s p a) c -> s p a c", s=2, p=P)
 
     with ExitStack() as ctx:
         keep = ctx.enter_context(tc.tile_pool(name="keep", bufs=1))
         work = ctx.enter_context(tc.tile_pool(name="work", bufs=2))
-        psum = ctx.enter_context(tc.psum_pool(name="psum", bufs=2))
+        psum = ctx.enter_context(tc.psum_pool(name="psum", bufs=BANKS))
         ctx.enter_context(tc.manual_schedule())
 
         ident = keep.tile([P, P], F32)
@@ -69,54 +78,75 @@ def tile_fermilayer_pa_v_kernel(
         dz_scales = [keep.tile([P, D_ONE], U8, align_bytes=64, name="dz_scales%d" % g) for g in range(PASSES)]
         in_codes = [keep.tile([P, K_IN], U32, align_bytes=64, name="in_codes%d" % g) for g in range(PASSES)]
         in_scales = [keep.tile([P, K_IN], U8, align_bytes=64, name="in_scales%d" % g) for g in range(PASSES)]
+        w_sb = keep.tile([P, F_BLOCKS * D_ONE], BF16)
 
         z_sb, grad_sb, h_sb, pair_sb = {}, {}, {}, {}
-        dz_sb, dz_tok, dz_feat, dzt_codes, dzt_scales = {}, {}, {}, {}, {}
-        part_sb, mean_t, back_ps, mean_tok, h_tok = {}, {}, {}, {}, {}
+        dz_sb, dz_tok, dz_feat, dzt_codes, dzt_scales, d_pair = {}, {}, {}, {}, {}, {}
+        part_sb, mean_t, back_bank, mean_tok, h_tok, w_grouped = {}, {}, {}, {}, {}, {}
+
+        def tile_16k(shape, dtype, name):
+            return work.tile(shape, dtype, tag="slot16k", bufs=CHUNKS, name=name)
+
+        def tile_8k(shape, dtype, name):
+            return work.tile(shape, dtype, tag="slot8k", bufs=PASSES, name=name)
+
+        def tile_4k(shape, dtype, name):
+            return work.tile(shape, dtype, tag="slot4k", bufs=2 * PASSES, name=name)
+
+        def grouped_tile(name):
+            return work.tile([P, ROW], BF16, tag="grouped", bufs=3, align_bytes=64, name=name)
+
+        def bank_tile(name):
+            return psum.tile([P, BANK], F32, tag="bank", name=name)
 
         def load_z(g):
-            z_sb[g] = work.tile([P, PACK * D_ONE], F32, tag="wide", bufs=PASSES, name="z_sb")
+            z_sb[g] = tile_8k([P, ROW], F32, "z_sb")
             nc.sync.dma_start(out=z_sb[g][:], in_=z_hbm[g])
 
         def load_grad(g):
-            grad_sb[g] = work.tile([P, PACK * D_ONE], BF16, tag="narrow", bufs=2 * PASSES, name="grad_sb")
+            grad_sb[g] = tile_4k([P, ROW], BF16, "grad_sb")
             nc.sync.dma_start(out=grad_sb[g][:], in_=grad_hbm[g])
 
         def load_h(g):
-            h_sb[g] = work.tile([P, PACK * D_ONE], BF16, tag="narrow", bufs=2 * PASSES, name="h_sb")
+            h_sb[g] = tile_4k([P, ROW], BF16, "h_sb")
             nc.sync.dma_start(out=h_sb[g][:], in_=h_hbm[g])
 
-        def load_pair(n):
-            stream, g, u = n // (2 * PASSES), n // 2 % PASSES, n % 2
-            pair_sb[n] = work.tile([P, 2 * N_SPIN * D_TWO], BF16, tag="pair", bufs=PAIR_BUFS, name="pair_sb")
-            nc.sync.dma_start(out=pair_sb[n][:], in_=pair_hbm[stream][g, u])
+        def load_weight(g):
+            nc.sync.dma_start(out=w_sb[:], in_=w_hbm)
 
-        def grouped_tile(name):
-            grouped = work.tile([P, PACK * D_ONE], BF16, tag="grouped", bufs=3, align_bytes=64, name=name)
-            return grouped
+        def load_pair(chunk, first, last):
+            stream, g = divmod(chunk, PASSES)
+            if first == 0:
+                pair_sb[chunk] = tile_16k([P, 2 * HALF], BF16, "pair_sb")
+            cols = slice(first * HALF, last * HALF)
+            nc.sync.dma_start(out=pair_sb[chunk][:, cols], in_=pair_hbm[stream][g][:, cols])
 
-        def weight_operand(w_sb):
-            words = w_sb[:].rearrange("p a k -> p (a k)").bitcast(F32)
-            bank = psum.tile([P, BANK], F32, tag="turn", name="w_bank")
+        def transpose_words(bank, words, row, place):
+            for u in range(2):
+                col = (2 * place + u) * P
+                nc.tensor.transpose(bank[:, col : col + P], words[:, 2 * P * row + u : 2 * P * (row + 1) : 2], ident[:])
+
+        def weight_layout():
+            bank = bank_tile("w_bank")
             for a in range(F_BLOCKS):
-                for u in range(2):
-                    col = (2 * a + u) * P
-                    nc.tensor.transpose(bank[:, col : col + P], words[:, 2 * P * a + u : 2 * P * (a + 1) : 2], ident[:])
-            w_grouped = grouped_tile("w_grouped")
+                transpose_words(bank, w_sb[:].bitcast(F32), a, a)
+            w_grouped[0] = grouped_tile("w_grouped")
             for rep in range(2):
-                dst = w_grouped[:].bitcast(F32)[:, rep * BANK : (rep + 1) * BANK]
+                dst = w_grouped[0][:].bitcast(F32)[:, rep * BANK : (rep + 1) * BANK]
                 nc.scalar.copy(
-                    out=dst.rearrange("p (a r u) -> p a r u", a=F_BLOCKS, u=2),
-                    in_=bank[:].rearrange("p (a u r) -> p a r u", a=F_BLOCKS, u=2),
+                    out=dst.rearrange("p (r a u) -> p r a u", a=F_BLOCKS, u=2),
+                    in_=bank[:].rearrange("p (a u r) -> p r a u", a=F_BLOCKS, u=2),
                 )
-            return w_grouped
+
+        def weight_quantize():
+            nc.vector.quantize_mx(out=w_codes[:].bitcast(E4M3), scales=w_scales[:], in_=w_grouped[0][:])
 
         def dz_activations(g):
             nc.scalar.activation(out=z_sb[g][:], in_=z_sb[g][:], func=ACT.Tanh, scale=1.0 / math.sqrt(2.0))
             nc.scalar.activation(out=z_sb[g][:], in_=z_sb[g][:], func=ACT.Square, scale=math.sqrt(DZ_GAIN))
 
         def dz_round(g):
-            dz_sb[g] = work.tile([P, PACK * D_ONE], BF16, tag="dz", name="dz_sb")
+            dz_sb[g] = work.tile([P, ROW], BF16, tag="dz", name="dz_sb")
             nc.vector.scalar_tensor_tensor(
                 out=dz_sb[g][:], in0=z_sb[g][:], scalar=DZ_GAIN, in1=grad_sb[g][:], op0=ALU.subtract, op1=ALU.mult
             )
@@ -127,18 +157,12 @@ def tile_fermilayer_pa_v_kernel(
                 out=dz_tok[g][:].rearrange("p (c j) -> p c j", j=PACK),
                 in_=dz_sb[g][:].rearrange("p (j c) -> p c j", j=PACK),
             )
-            words = dz_sb[g][:].bitcast(F32)
             dz_feat[g] = grouped_tile("dz_feat")
-            for half in range(2):
-                bank = psum.tile([P, BANK], F32, tag="turn", name="dz_bank")
+            for u_tok in range(2):
+                bank = bank_tile("dz_bank")
                 for e in range(2):
-                    j = 2 * half + e
-                    for u in range(2):
-                        col = (2 * e + u) * P
-                        nc.tensor.transpose(
-                            bank[:, col : col + P], words[:, 2 * P * j + u : 2 * P * (j + 1) : 2], ident[:]
-                        )
-                dst = dz_feat[g][:].bitcast(F32)[:, half * BANK : (half + 1) * BANK]
+                    transpose_words(bank, dz_sb[g][:].bitcast(F32), 2 * u_tok + e, e)
+                dst = dz_feat[g][:].bitcast(F32)[:, u_tok * BANK : (u_tok + 1) * BANK]
                 nc.scalar.copy(
                     out=dst.rearrange("p (e r u) -> p e r u", e=2, u=2),
                     in_=bank[:].rearrange("p (e u r) -> p e r u", e=2, u=2),
@@ -146,14 +170,15 @@ def tile_fermilayer_pa_v_kernel(
 
         def dz_quantize(g):
             nc.vector.quantize_mx(out=dz_codes[g][:].bitcast(E5M2), scales=dz_scales[g][:], in_=dz_tok[g][:])
-            dzt_codes[g] = work.tile([P, K_PASS], U32, tag="dzt_codes", align_bytes=64, name="dzt_codes")
-            dzt_scales[g] = work.tile([P, K_PASS], U8, tag="dzt_scales", align_bytes=64, name="dzt_scales")
+            dzt_codes[g] = work.tile([P, PACK * P], U32, tag="dzt_codes", bufs=PASSES, align_bytes=64, name="dzt_codes")
+            dzt_scales[g] = work.tile([P, PACK * P], U8, tag="dzt_scales", bufs=PASSES, align_bytes=64, name="dzt_scales")
             nc.vector.quantize_mx(out=dzt_codes[g][:].bitcast(E5M2), scales=dzt_scales[g][:], in_=dz_feat[g][:])
 
-        def pair_gradient(g):
-            result = work.tile([P, PACK * BANK], F32, tag="wide", bufs=PASSES, name="d_pair")
-            for j in range(PACK):
-                acc = psum.tile([P, BANK], F32, tag="mx", name="acc0")
+        def pair_gradient(g, u):
+            if u == 0:
+                d_pair[g] = tile_16k([P, PACK * COPIES * D_TWO], F32, "d_pair")
+            for j in (2 * u, 2 * u + 1):
+                acc = bank_tile("acc0")
                 nc.tensor.matmul_mx(
                     out=acc[:],
                     lhsT=dzt_codes[g][:, j * P : (j + 1) * P].bitcast(E5M2),
@@ -163,57 +188,68 @@ def tile_fermilayer_pa_v_kernel(
                     start=True,
                     stop=True,
                 )
-                twice = result[:, j * BANK : (j + 1) * BANK]
-                nc.scalar.activation(out=twice, in_=acc[:], func=ACT.Copy, scale=-1.0 / N_SPIN)
-                nc.sync.dma_start(out=out0_hbm[g, j], in_=twice.unsqueeze(1).to_broadcast([P, N_SPIN // 2, BANK]))
+                first = j * COPIES * D_TWO
+                nc.scalar.activation(out=d_pair[g][:, first : first + BANK], in_=acc[:], func=ACT.Copy, scale=-1.0 / N_SPIN)
 
-        def pair_add(n):
-            rows = pair_sb[n][:].rearrange("p (e h x) -> p e h x", e=2, h=2)
-            part_sb[n] = work.tile([P, 2, HALF_ROWS * D_TWO], F32, tag="part", bufs=3, name="part_sb")
-            nc.vector.tensor_tensor(out=part_sb[n][:], in0=rows[:, :, 0, :], in1=rows[:, :, 1, :], op=ALU.add)
+        def pair_gradient_store(g, u):
+            for j in (2 * u, 2 * u + 1):
+                first = j * COPIES * D_TWO
+                nc.vector.tensor_copy(out=d_pair[g][:, first + BANK : first + 2 * BANK], in_=d_pair[g][:, first : first + BANK])
+                rows = d_pair[g][:, first : first + COPIES * D_TWO]
+                nc.sync.dma_start(
+                    out=out0_hbm[g, j], in_=rows.unsqueeze(1).to_broadcast([P, N_SPIN // COPIES, COPIES * D_TWO])
+                )
 
-        def pair_mean(n):
-            bank = psum.tile([P, BANK], F32, tag="sum", name="sum_bank")
+        def pair_add(half):
+            chunk, u = divmod(half, 2)
+            rows = pair_sb[chunk][:, u * HALF : (u + 1) * HALF].rearrange("p (e v x) -> p e v x", e=2, v=2)
+            part_sb[half] = work.tile([P, 2, PARTS * D_TWO], F32, tag="part", bufs=3, name="part_sb")
+            nc.vector.tensor_tensor(out=part_sb[half][:], in0=rows[:, :, 0, :], in1=rows[:, :, 1, :], op=ALU.add)
+
+        def pair_mean(half):
+            bank = bank_tile("sum_bank")
             for b in range(F_BLOCKS):
                 for e in range(2):
                     col = (2 * b + e) * P
-                    for r in range(HALF_ROWS):
+                    for r in range(PARTS):
                         first = r * D_TWO + b * P
                         nc.tensor.matmul(
                             bank[:, col : col + P],
-                            lhsT=part_sb[n][:, e, first : first + P],
+                            lhsT=part_sb[half][:, e, first : first + P],
                             rhs=ident[:],
                             is_transpose=True,
                             start=(r == 0),
-                            stop=(r == HALF_ROWS - 1),
+                            stop=(r == PARTS - 1),
                         )
-            mean_t[n] = work.tile([P, BANK], BF16, tag="mean_t", name="mean_t")
+            mean_t[half] = work.tile([P, BANK], BF16, tag="mean_t", bufs=3, name="mean_t")
             nc.scalar.activation(
-                out=mean_t[n][:].rearrange("p (b q e) -> p b q e", b=F_BLOCKS, e=2),
+                out=mean_t[half][:].rearrange("p (b q e) -> p b q e", b=F_BLOCKS, e=2),
                 in_=bank[:].rearrange("p (b e q) -> p b q e", b=F_BLOCKS, e=2),
                 func=ACT.Copy,
                 scale=1.0 / N_SPIN,
             )
 
-        def pair_turn_back(n):
-            k, u = divmod(n, 2)
+        def pair_turn_back(half):
+            chunk, u = divmod(half, 2)
             if u == 0:
-                back_ps[k] = psum.tile([P, BANK], F32, tag="back", name="back_bank")
-            words = mean_t[n][:].bitcast(F32)
+                back_bank[chunk] = bank_tile("back_bank")
+            words = mean_t[half][:].bitcast(F32)
             for b in range(F_BLOCKS):
                 col = u * D_TWO + b * P
-                nc.tensor.transpose(back_ps[k][:, col : col + P], words[:, b * P : (b + 1) * P], ident[:])
+                nc.tensor.transpose(back_bank[chunk][:, col : col + P], words[:, b * P : (b + 1) * P], ident[:])
             if u == 1:
-                mean_tok[k] = work.tile([P, PACK * D_TWO], BF16, tag="mean_tok", align_bytes=64, name="mean_tok")
+                mean_tok[chunk] = work.tile([P, PACK * D_TWO], BF16, tag="mean_tok", align_bytes=64, name="mean_tok")
                 nc.scalar.copy(
-                    out=mean_tok[k][:].bitcast(F32).rearrange("p (f u) -> p f u", u=2),
-                    in_=back_ps[k][:].rearrange("p (u f) -> p f u", u=2),
+                    out=mean_tok[chunk][:].bitcast(F32).rearrange("p (a m u) -> p a m u", a=2, u=2),
+                    in_=back_bank[chunk][:].rearrange("p (u m a) -> p a m u", a=2, u=2),
                 )
 
-        def pair_quantize(k):
-            stream, g = divmod(k, PASSES)
+        def pair_quantize(chunk):
+            stream, g = divmod(chunk, PASSES)
             cols = slice(D_ONE + stream * D_TWO, D_ONE + (stream + 1) * D_TWO)
-            nc.vector.quantize_mx(out=in_codes[g][:, cols].bitcast(E4M3), scales=in_scales[g][:, cols], in_=mean_tok[k][:])
+            nc.vector.quantize_mx(
+                out=in_codes[g][:, cols].bitcast(E4M3), scales=in_scales[g][:, cols], in_=mean_tok[chunk][:]
+            )
 
         def h_interleave(g):
             h_tok[g] = grouped_tile("h_tok")
@@ -227,11 +263,10 @@ def tile_fermilayer_pa_v_kernel(
                 out=in_codes[g][:, :D_ONE].bitcast(E4M3), scales=in_scales[g][:, :D_ONE], in_=h_tok[g][:]
             )
 
-        def weight_gradient(q):
-            result = work.tile([P, 2, D_ONE], F32, tag="narrow", bufs=2 * PASSES, name="d_w")
-            for a in range(2):
-                cols = slice((2 * q + a) * P, (2 * q + a + 1) * P)
-                acc = psum.tile([P, BANK], F32, tag="mx", name="acc1")
+        def weight_gradient(first, result, dest):
+            for a in range(result.shape[1]):
+                cols = slice(first + a * P, first + (a + 1) * P)
+                acc = bank_tile("acc1")
                 for g in range(PASSES):
                     nc.tensor.matmul_mx(
                         out=acc[:],
@@ -243,47 +278,51 @@ def tile_fermilayer_pa_v_kernel(
                         stop=(g == PASSES - 1),
                     )
                 nc.scalar.activation(out=result[:, a, :], in_=acc[:], func=ACT.Copy, scale=-1.0)
-            nc.sync.dma_start(out=out1_hbm[q], in_=result[:])
+            nc.sync.dma_start(out=dest, in_=result[:])
 
-        w_sb = keep.tile([P, F_BLOCKS, D_ONE], BF16)
-        for g in range(PASSES):
-            load_pair(2 * g)
-            load_z(g)
-            load_grad(g)
-            if g == 0:
-                nc.sync.dma_start(out=w_sb[:], in_=w_hbm)
-            load_pair(2 * g + 1)
+        def weight_gradient_pair(stream):
+            weight_gradient(D_ONE + stream * D_TWO, tile_4k([P, F_BLOCKS, D_ONE], F32, "d_w_pair"), out1_pair[stream])
+
+        between = [(load_z, 0), (load_grad, 0), (load_weight, 0)]
+        between.extend((load, g) for g in range(1, PASSES) for load in (load_z, load_grad))
+        for half in range(len(between) + 1):
+            load_pair(half // 2, half % 2, half % 2 + 1)
+            if half < len(between):
+                between[half][0](between[half][1])
         for g in range(PASSES):
             load_h(g)
-        for n in range(2 * PASSES, PAIR_BUFS):
-            load_pair(n)
+        for chunk in range((len(between) + 1) // 2, CHUNKS):
+            load_pair(chunk, 0, 2)
 
-        dz_stages = [dz_activations, dz_round, dz_layouts, dz_quantize, pair_gradient]
-        h_first = 2 * PASSES + 1
-        for step in range(CHUNKS + 3):
-            if step % 2 == 0 and step // 2 < PASSES:
-                dz_activations(step // 2)
-            if step < CHUNKS:
+        dz_stages = {0: dz_activations, DZ_LEAD: dz_round, DZ_LEAD + 1: dz_layouts, DZ_LEAD + 2: dz_quantize}
+        out0_first = DZ_FIRST + DZ_LEAD + 3
+        out1_first = H_FIRST + PASSES + 1
+        for step in range(HALVES + 3):
+            if step < HALVES:
                 pair_add(step)
-            if step + PAIR_BUFS < CHUNKS:
-                load_pair(step + PAIR_BUFS)
-            if 0 <= step - 1 < CHUNKS:
+            if 0 <= step - out0_first - 1 < 2 * PASSES:
+                pair_gradient_store(*divmod(step - out0_first - 1, 2))
+            if step == W_STEP:
+                weight_layout()
+            if 0 <= step - 1 < HALVES:
                 pair_mean(step - 1)
-            if 0 <= step - 2 < CHUNKS:
+            if 0 <= step - 2 < HALVES:
                 pair_turn_back(step - 2)
-            if 0 <= step - 3 < CHUNKS and (step - 3) % 2 == 1:
+            if 0 <= step - 3 < HALVES and (step - 3) % 2 == 1:
                 pair_quantize((step - 3) // 2)
-            if step == 0:
-                w_grouped = weight_operand(w_sb)
-            if step == 1:
-                nc.vector.quantize_mx(out=w_codes[:].bitcast(E4M3), scales=w_scales[:], in_=w_grouped[:])
+            if step == W_STEP + 1:
+                weight_quantize()
+            if 0 <= step - H_FIRST - 1 < PASSES:
+                h_quantize(step - H_FIRST - 1)
+            if 0 <= step - out0_first < 2 * PASSES:
+                pair_gradient(*divmod(step - out0_first, 2))
             for g in range(PASSES):
-                if 1 <= step - 2 * g < len(dz_stages):
-                    dz_stages[step - 2 * g](g)
-            if 0 <= step - h_first - 1 < PASSES:
-                h_quantize(step - h_first - 1)
-            if 0 <= step - h_first < PASSES:
-                h_interleave(step - h_first)
-            if 0 <= step - h_first - PASSES - 1 < 3:
-                weight_gradient(step - h_first - PASSES - 1)
-        weight_gradient(3)
+                if step - DZ_FIRST - 2 * g in dz_stages:
+                    dz_stages[step - DZ_FIRST - 2 * g](g)
+            if 0 <= step - H_FIRST < PASSES:
+                h_interleave(step - H_FIRST)
+            if step == out1_first:
+                weight_gradient(0, tile_8k([P, PACK, D_ONE], F32, "d_w_h"), out1_h)
+            if step == out1_first + 1:
+                weight_gradient_pair(0)
+        weight_gradient_pair(1)

import math
from contextlib import ExitStack

import concourse.mybir as mybir
from concourse.masks import make_identity

N_ELEC, N_SPIN, D_ONE, D_TWO = 1536, 8, 512, 256
K_IN = D_ONE + 2 * D_TWO
DZ_GAIN = 0.5 * 1.5927812698663606

FLOPS = 2 * N_ELEC * D_ONE * D_TWO + 2 * N_ELEC * K_IN * D_ONE
BYTES = (
    2 * N_ELEC * D_ONE * 2
    + N_ELEC * D_ONE * 4
    + 2 * N_ELEC * N_SPIN * D_TWO * 2
    + D_TWO * D_ONE * 2
    + N_ELEC * N_SPIN * D_TWO * 4
    + K_IN * D_ONE * 4
)

F32 = mybir.dt.float32
BF16 = mybir.dt.bfloat16
U32 = mybir.dt.uint32
U8 = mybir.dt.uint8
E4M3 = mybir.dt.float8_e4m3fn_x4
E5M2 = mybir.dt.float8_e5m2_x4
ACT = mybir.ActivationFunctionType
ALU = mybir.AluOpType

P = 128
PACK = 4
PASSES = N_ELEC // (P * PACK)
BANK = 512
BANKS = 8
F_BLOCKS = D_TWO // P
PARTS = N_SPIN // 2
ROW = PACK * D_ONE

CHUNKS = 2 * PASSES
HALVES = 2 * CHUNKS
HALF = 2 * N_SPIN * D_TWO
COPIES = 4

DZ_FIRST = 1
DZ_LEAD = 2
W_STEP = 2
H_FIRST = 8


def tile_fermilayer_pa_v_kernel(
    tc, h_one, h_two_same, h_two_diff, W1, b1, Wg, z, grad_out, out_0, out_1
):
    nc = tc.nc

    z_hbm = z.rearrange("(g p j) c -> g p (j c)", p=P, j=PACK)
    grad_hbm = grad_out.rearrange("(g p j) c -> g p (j c)", p=P, j=PACK)
    h_hbm = h_one.rearrange("(g p j) c -> g p (j c)", p=P, j=PACK)
    pair_hbm = [
        stream.rearrange("(g p x) f -> g p (x f)", p=P, x=PACK * N_SPIN) for stream in (h_two_same, h_two_diff)
    ]
    w_hbm = W1[D_ONE : D_ONE + D_TWO, :].rearrange("(r a) k -> r (a k)", r=P)
    out0_hbm = out_0.rearrange("(g p j q r) f -> g j p q (r f)", p=P, j=PACK, q=N_SPIN // COPIES, r=COPIES)
    out1_h = out_1[:D_ONE, :].rearrange("(a p) c -> p a c", p=P)
    out1_pair = out_1[D_ONE:, :].rearrange("(s p a) c -> s p a c", s=2, p=P)

    with ExitStack() as ctx:
        keep = ctx.enter_context(tc.tile_pool(name="keep", bufs=1))
        work = ctx.enter_context(tc.tile_pool(name="work", bufs=2))
        psum = ctx.enter_context(tc.psum_pool(name="psum", bufs=BANKS))
        ctx.enter_context(tc.manual_schedule())

        ident = keep.tile([P, P], F32)
        make_identity(nc, ident[:])

        w_codes = keep.tile([P, BANK], U32, align_bytes=64)
        w_scales = keep.tile([P, BANK], U8, align_bytes=64)
        dz_codes = [keep.tile([P, D_ONE], U32, align_bytes=64, name="dz_codes%d" % g) for g in range(PASSES)]
        dz_scales = [keep.tile([P, D_ONE], U8, align_bytes=64, name="dz_scales%d" % g) for g in range(PASSES)]
        in_codes = [keep.tile([P, K_IN], U32, align_bytes=64, name="in_codes%d" % g) for g in range(PASSES)]
        in_scales = [keep.tile([P, K_IN], U8, align_bytes=64, name="in_scales%d" % g) for g in range(PASSES)]
        w_sb = keep.tile([P, F_BLOCKS * D_ONE], BF16)

        z_sb, grad_sb, h_sb, pair_sb = {}, {}, {}, {}
        dz_sb, dz_tok, dz_feat, dzt_codes, dzt_scales, d_pair = {}, {}, {}, {}, {}, {}
        part_sb, mean_t, back_bank, mean_tok, h_tok, w_grouped = {}, {}, {}, {}, {}, {}

        def tile_16k(shape, dtype, name):
            return work.tile(shape, dtype, tag="slot16k", bufs=CHUNKS, name=name)

        def tile_8k(shape, dtype, name):
            return work.tile(shape, dtype, tag="slot8k", bufs=PASSES, name=name)

        def tile_4k(shape, dtype, name):
            return work.tile(shape, dtype, tag="slot4k", bufs=2 * PASSES, name=name)

        def grouped_tile(name):
            return work.tile([P, ROW], BF16, tag="grouped", bufs=3, align_bytes=64, name=name)

        def bank_tile(name):
            return psum.tile([P, BANK], F32, tag="bank", name=name)

        def load_z(g):
            z_sb[g] = tile_8k([P, ROW], F32, "z_sb")
            nc.sync.dma_start(out=z_sb[g][:], in_=z_hbm[g])

        def load_grad(g):
            grad_sb[g] = tile_4k([P, ROW], BF16, "grad_sb")
            nc.sync.dma_start(out=grad_sb[g][:], in_=grad_hbm[g])

        def load_h(g):
            h_sb[g] = tile_4k([P, ROW], BF16, "h_sb")
            nc.sync.dma_start(out=h_sb[g][:], in_=h_hbm[g])

        def load_weight(g):
            nc.sync.dma_start(out=w_sb[:], in_=w_hbm)

        def load_pair(chunk, first, last):
            stream, g = divmod(chunk, PASSES)
            if first == 0:
                pair_sb[chunk] = tile_16k([P, 2 * HALF], BF16, "pair_sb")
            cols = slice(first * HALF, last * HALF)
            nc.sync.dma_start(out=pair_sb[chunk][:, cols], in_=pair_hbm[stream][g][:, cols])

        def transpose_words(bank, words, row, place):
            for u in range(2):
                col = (2 * place + u) * P
                nc.tensor.transpose(bank[:, col : col + P], words[:, 2 * P * row + u : 2 * P * (row + 1) : 2], ident[:])

        def weight_layout():
            bank = bank_tile("w_bank")
            for a in range(F_BLOCKS):
                transpose_words(bank, w_sb[:].bitcast(F32), a, a)
            w_grouped[0] = grouped_tile("w_grouped")
            for rep in range(2):
                dst = w_grouped[0][:].bitcast(F32)[:, rep * BANK : (rep + 1) * BANK]
                nc.scalar.copy(
                    out=dst.rearrange("p (r a u) -> p r a u", a=F_BLOCKS, u=2),
                    in_=bank[:].rearrange("p (a u r) -> p r a u", a=F_BLOCKS, u=2),
                )

        def weight_quantize():
            nc.vector.quantize_mx(out=w_codes[:].bitcast(E4M3), scales=w_scales[:], in_=w_grouped[0][:])

        def dz_activations(g):
            nc.scalar.activation(out=z_sb[g][:], in_=z_sb[g][:], func=ACT.Tanh, scale=1.0 / math.sqrt(2.0))
            nc.scalar.activation(out=z_sb[g][:], in_=z_sb[g][:], func=ACT.Square, scale=math.sqrt(DZ_GAIN))

        def dz_round(g):
            dz_sb[g] = work.tile([P, ROW], BF16, tag="dz", name="dz_sb")
            nc.vector.scalar_tensor_tensor(
                out=dz_sb[g][:], in0=z_sb[g][:], scalar=DZ_GAIN, in1=grad_sb[g][:], op0=ALU.subtract, op1=ALU.mult
            )

        def dz_layouts(g):
            dz_tok[g] = grouped_tile("dz_tok")
            nc.vector.tensor_copy(
                out=dz_tok[g][:].rearrange("p (c j) -> p c j", j=PACK),
                in_=dz_sb[g][:].rearrange("p (j c) -> p c j", j=PACK),
            )
            dz_feat[g] = grouped_tile("dz_feat")
            for u_tok in range(2):
                bank = bank_tile("dz_bank")
                for e in range(2):
                    transpose_words(bank, dz_sb[g][:].bitcast(F32), 2 * u_tok + e, e)
                dst = dz_feat[g][:].bitcast(F32)[:, u_tok * BANK : (u_tok + 1) * BANK]
                nc.scalar.copy(
                    out=dst.rearrange("p (e r u) -> p e r u", e=2, u=2),
                    in_=bank[:].rearrange("p (e u r) -> p e r u", e=2, u=2),
                )

        def dz_quantize(g):
            nc.vector.quantize_mx(out=dz_codes[g][:].bitcast(E5M2), scales=dz_scales[g][:], in_=dz_tok[g][:])
            dzt_codes[g] = work.tile([P, PACK * P], U32, tag="dzt_codes", bufs=PASSES, align_bytes=64, name="dzt_codes")
            dzt_scales[g] = work.tile([P, PACK * P], U8, tag="dzt_scales", bufs=PASSES, align_bytes=64, name="dzt_scales")
            nc.vector.quantize_mx(out=dzt_codes[g][:].bitcast(E5M2), scales=dzt_scales[g][:], in_=dz_feat[g][:])

        def pair_gradient(g, u):
            if u == 0:
                d_pair[g] = tile_16k([P, PACK * COPIES * D_TWO], F32, "d_pair")
            for j in (2 * u, 2 * u + 1):
                acc = bank_tile("acc0")
                nc.tensor.matmul_mx(
                    out=acc[:],
                    lhsT=dzt_codes[g][:, j * P : (j + 1) * P].bitcast(E5M2),
                    lhsT_scale=dzt_scales[g][:, j * P : (j + 1) * P],
                    rhs=w_codes[:].bitcast(E4M3),
                    rhs_scale=w_scales[:],
                    start=True,
                    stop=True,
                )
                first = j * COPIES * D_TWO
                nc.scalar.activation(out=d_pair[g][:, first : first + BANK], in_=acc[:], func=ACT.Copy, scale=-1.0 / N_SPIN)

        def pair_gradient_store(g, u):
            for j in (2 * u, 2 * u + 1):
                first = j * COPIES * D_TWO
                nc.vector.tensor_copy(out=d_pair[g][:, first + BANK : first + 2 * BANK], in_=d_pair[g][:, first : first + BANK])
                rows = d_pair[g][:, first : first + COPIES * D_TWO]
                nc.sync.dma_start(
                    out=out0_hbm[g, j], in_=rows.unsqueeze(1).to_broadcast([P, N_SPIN // COPIES, COPIES * D_TWO])
                )

        def pair_add(half):
            chunk, u = divmod(half, 2)
            rows = pair_sb[chunk][:, u * HALF : (u + 1) * HALF].rearrange("p (e v x) -> p e v x", e=2, v=2)
            part_sb[half] = work.tile([P, 2, PARTS * D_TWO], F32, tag="part", bufs=3, name="part_sb")
            nc.vector.tensor_tensor(out=part_sb[half][:], in0=rows[:, :, 0, :], in1=rows[:, :, 1, :], op=ALU.add)

        def pair_mean(half):
            bank = bank_tile("sum_bank")
            for b in range(F_BLOCKS):
                for e in range(2):
                    col = (2 * b + e) * P
                    for r in range(PARTS):
                        first = r * D_TWO + b * P
                        nc.tensor.matmul(
                            bank[:, col : col + P],
                            lhsT=part_sb[half][:, e, first : first + P],
                            rhs=ident[:],
                            is_transpose=True,
                            start=(r == 0),
                            stop=(r == PARTS - 1),
                        )
            mean_t[half] = work.tile([P, BANK], BF16, tag="mean_t", bufs=3, name="mean_t")
            nc.scalar.activation(
                out=mean_t[half][:].rearrange("p (b q e) -> p b q e", b=F_BLOCKS, e=2),
                in_=bank[:].rearrange("p (b e q) -> p b q e", b=F_BLOCKS, e=2),
                func=ACT.Copy,
                scale=1.0 / N_SPIN,
            )

        def pair_turn_back(half):
            chunk, u = divmod(half, 2)
            if u == 0:
                back_bank[chunk] = bank_tile("back_bank")
            words = mean_t[half][:].bitcast(F32)
            for b in range(F_BLOCKS):
                col = u * D_TWO + b * P
                nc.tensor.transpose(back_bank[chunk][:, col : col + P], words[:, b * P : (b + 1) * P], ident[:])
            if u == 1:
                mean_tok[chunk] = work.tile([P, PACK * D_TWO], BF16, tag="mean_tok", align_bytes=64, name="mean_tok")
                nc.scalar.copy(
                    out=mean_tok[chunk][:].bitcast(F32).rearrange("p (a m u) -> p a m u", a=2, u=2),
                    in_=back_bank[chunk][:].rearrange("p (u m a) -> p a m u", a=2, u=2),
                )

        def pair_quantize(chunk):
            stream, g = divmod(chunk, PASSES)
            cols = slice(D_ONE + stream * D_TWO, D_ONE + (stream + 1) * D_TWO)
            nc.vector.quantize_mx(
                out=in_codes[g][:, cols].bitcast(E4M3), scales=in_scales[g][:, cols], in_=mean_tok[chunk][:]
            )

        def h_interleave(g):
            h_tok[g] = grouped_tile("h_tok")
            nc.scalar.copy(
                out=h_tok[g][:].rearrange("p (c j) -> p c j", j=PACK),
                in_=h_sb[g][:].rearrange("p (j c) -> p c j", j=PACK),
            )

        def h_quantize(g):
            nc.vector.quantize_mx(
                out=in_codes[g][:, :D_ONE].bitcast(E4M3), scales=in_scales[g][:, :D_ONE], in_=h_tok[g][:]
            )

        def weight_gradient(first, result, dest):
            for a in range(result.shape[1]):
                cols = slice(first + a * P, first + (a + 1) * P)
                acc = bank_tile("acc1")
                for g in range(PASSES):
                    nc.tensor.matmul_mx(
                        out=acc[:],
                        lhsT=in_codes[g][:, cols].bitcast(E4M3),
                        lhsT_scale=in_scales[g][:, cols],
                        rhs=dz_codes[g][:].bitcast(E5M2),
                        rhs_scale=dz_scales[g][:],
                        start=(g == 0),
                        stop=(g == PASSES - 1),
                    )
                nc.scalar.activation(out=result[:, a, :], in_=acc[:], func=ACT.Copy, scale=-1.0)
            nc.sync.dma_start(out=dest, in_=result[:])

        def weight_gradient_pair(stream):
            weight_gradient(D_ONE + stream * D_TWO, tile_4k([P, F_BLOCKS, D_ONE], F32, "d_w_pair"), out1_pair[stream])

        between = [(load_z, 0), (load_grad, 0), (load_weight, 0)]
        between.extend((load, g) for g in range(1, PASSES) for load in (load_z, load_grad))
        for half in range(len(between) + 1):
            load_pair(half // 2, half % 2, half % 2 + 1)
            if half < len(between):
                between[half][0](between[half][1])
        for g in range(PASSES):
            load_h(g)
        for chunk in range((len(between) + 1) // 2, CHUNKS):
            load_pair(chunk, 0, 2)

        dz_stages = {0: dz_activations, DZ_LEAD: dz_round, DZ_LEAD + 1: dz_layouts, DZ_LEAD + 2: dz_quantize}
        out0_first = DZ_FIRST + DZ_LEAD + 3
        out1_first = H_FIRST + PASSES + 1
        for step in range(HALVES + 3):
            if step < HALVES:
                pair_add(step)
            if 0 <= step - out0_first - 1 < 2 * PASSES:
                pair_gradient_store(*divmod(step - out0_first - 1, 2))
            if step == W_STEP:
                weight_layout()
            if 0 <= step - 1 < HALVES:
                pair_mean(step - 1)
            if 0 <= step - 2 < HALVES:
                pair_turn_back(step - 2)
            if 0 <= step - 3 < HALVES and (step - 3) % 2 == 1:
                pair_quantize((step - 3) // 2)
            if step == W_STEP + 1:
                weight_quantize()
            if 0 <= step - H_FIRST - 1 < PASSES:
                h_quantize(step - H_FIRST - 1)
            if 0 <= step - out0_first < 2 * PASSES:
                pair_gradient(*divmod(step - out0_first, 2))
            for g in range(PASSES):
                if step - DZ_FIRST - 2 * g in dz_stages:
                    dz_stages[step - DZ_FIRST - 2 * g](g)
            if 0 <= step - H_FIRST < PASSES:
                h_interleave(step - H_FIRST)
            if step == out1_first:
                weight_gradient(0, tile_8k([P, PACK, D_ONE], F32, "d_w_h"), out1_h)
            if step == out1_first + 1:
                weight_gradient_pair(0)
        weight_gradient_pair(1)
